import numpy as np
import ml_dtypes


def mxq(x, axis, fmt="e4m3"):
    dtype, down = {"e4m3": (ml_dtypes.float8_e4m3fn, 7), "e5m2": (ml_dtypes.float8_e5m2, 14)}[fmt]
    v = np.moveaxis(np.asarray(x, np.float32).astype(ml_dtypes.bfloat16).astype(np.float64), axis, -1)
    blocks = v.reshape(v.shape[:-1] + (-1, 32))
    amax = np.abs(blocks).max(-1, keepdims=True)
    byte = np.maximum(np.where(amax > 0, np.frexp(amax)[1] - 1 + 127, 0) - down, 1)
    scale = np.exp2(byte - 127.0)
    codes = (blocks / scale).astype(np.float32).astype(dtype).astype(np.float64)
    return np.moveaxis((codes * scale).reshape(v.shape), -1, axis)


WIDE = False


def mx_kscale(k):
    if not WIDE:
        return np.ones(k)
    levels = np.array([10, -10, 5, -5, 0])
    if k % 512:
        return np.exp2(np.random.permutation(np.resize(levels, k // 32))).repeat(32)
    a = np.empty((k // 512, 16))
    for p in range(k // 512):
        a[p, :8] = np.random.permutation(np.resize(levels, 8))
        for g in range(8):
            far = levels[np.abs(levels - a[p, g]) >= 10]
            a[p, g + 8] = far[np.random.randint(len(far))]
    return np.exp2(a.ravel()).repeat(32)


BF16 = ml_dtypes.bfloat16


def bf(x):
    return np.asarray(x, np.float32).astype(BF16)


def f64(x):
    return np.asarray(x).astype(np.float64)


B, A, E, H, NEXP, NACT = 128, 8, 512, 512, 8, 128
M = B * A


def sigmoid(v):
    return 1.0 / (1.0 + np.exp(-v))


def setup_inputs():
    s, t = mx_kscale(H), mx_kscale(H)
    return {
        "h": bf(np.random.standard_normal((M, H)) * 0.65 * s),
        "gate_logit": bf(np.random.standard_normal((M, NEXP))),
        "e_w1": bf(np.random.standard_normal((NEXP, H, H)) * 1.5 / np.sqrt(H) / s[None, None, :] * t[None, :, None]),
        "e_b1": bf(np.random.standard_normal((NEXP, H)) * 0.3 * t[None, :]),
        "e_w2": bf(np.random.standard_normal((NEXP, NACT, H)) * 2.0 / np.sqrt(H) / t[None, None, :]),
        "e_b2": bf(np.random.standard_normal((NEXP, NACT)) * 0.3),
    }


def reference(h, gate_logit, e_w1, e_b1, e_w2, e_b2):
    hq = mxq(f64(h), 1, "e4m3")
    h1 = np.maximum(f64(bf(hq @ mxq(f64(e_w1), 2, "e4m3").transpose(0, 2, 1))) + f64(e_b1)[:, None, :], 0.0)
    experts_out = (mxq(h1, 2, "e4m3") @ mxq(f64(e_w2), 2, "e4m3").transpose(0, 2, 1)) + f64(e_b2)[:, None, :]
    weight = sigmoid(f64(gate_logit))
    w = weight.T[:, :, None]
    final_q = (experts_out * w).mean(axis=0)
    return final_q, np.swapaxes(experts_out, 0, 1)

@@ -1,0 +1,285 @@
+from contextlib import ExitStack
+
+import concourse.mybir as mybir
+from concourse.masks import make_identity
+
+F32 = mybir.dt.float32
+BF16 = mybir.dt.bfloat16
+U32 = mybir.dt.uint32
+U8 = mybir.dt.uint8
+FP8X4 = mybir.dt.float8_e4m3fn_x4
+ACT = mybir.ActivationFunctionType
+ALU = mybir.AluOpType
+
+P = 128
+TOKENS = 1024
+HID = 512
+EXPERTS = 8
+ACTIONS = 128
+TILES = TOKENS // P
+HALF = 4
+UNITS = 2 * EXPERTS
+BANK_DT = BF16
+S_SHARE = 64
+
+FLOPS = 2 * TOKENS * HID * HID * EXPERTS + 2 * TOKENS * HID * ACTIONS * EXPERTS
+
+
+def tile_mspagent_pb_kernel(tc, h, gate_logit, e_w1, e_b1, e_w2, e_b2, out_0, out_1):
+    nc = tc.nc
+    with ExitStack() as ctx:
+        keep = ctx.enter_context(tc.tile_pool(name="keep", bufs=1))
+        work = ctx.enter_context(tc.tile_pool(name="work", bufs=2))
+        psum = ctx.enter_context(tc.psum_pool(name="psum", bufs=2))
+        ctx.enter_context(tc.manual_schedule())
+
+        warm = keep.tile([P, 1], F32, name="warm", tag="warm")
+        nc.gpsimd.memset(warm[:], 0.0)
+        ident = keep.tile([P, P], F32, name="ident", tag="ident")
+        make_identity(nc, ident[:])
+        b2row = keep.tile([P, EXPERTS * ACTIONS], BF16, name="b2row", tag="b2row")
+        nc.gpsimd.memset(b2row[:], 0.0)
+        ones = keep.tile([P, P], BF16, name="ones", tag="ones")
+        nc.gpsimd.memset(ones[:], 1.0)
+
+        b1 = keep.tile([P, EXPERTS, 4], BF16, name="b1", tag="b1")
+        nc.scalar.dma_start(out=b1[:], in_=e_b1.rearrange("e (m t) -> m e t", t=4))
+        gl = keep.tile([P, TILES * EXPERTS], BF16, name="gl", tag="gl")
+        nc.scalar.dma_start(out=gl[:], in_=gate_logit.rearrange("(p i) e -> p (i e)", i=TILES))
+        nc.scalar.activation(out=warm[:], in_=warm[:], func=ACT.Sigmoid)
+        nc.scalar.dma_start(out=b2row[0:1, :], in_=e_b2.rearrange("(o e) a -> o (e a)", o=1))
+
+        h_v = h.rearrange("(p i) k -> p i k", i=TILES)
+        rows = {}
+
+        def load_h(c):
+            t = keep.tile([P, 2, HID], BF16, name="h_sb%d" % c, tag="h_sb%d" % c)
+            nc.sync.dma_start(out=t[:], in_=h_v[:, 2 * c : 2 * c + 2, :])
+            rows.setdefault(("h", c // 2), []).extend([t[:, 0, :], t[:, 1, :]])
+
+        def load_w1(e, pieces):
+            w1_v = e_w1[e].rearrange("(m t) k -> m t k", t=4)
+            n = 4 // pieces
+            for c in range(pieces):
+                t = keep.tile([P, n, HID], BF16, name="w1_sb%d_%d" % (e, c), tag="w1_sb%d_%d" % (e, c))
+                nc.sync.dma_start(out=t[:], in_=w1_v[:, c * n : (c + 1) * n, :])
+                rows.setdefault(("w1", e), []).extend([t[:, x, :] for x in range(n)])
+
+        def load_w2(c):
+            t = keep.tile([P, 4, HID], BF16, name="w2_sb%d" % c, tag="w2_sb%d" % c)
+            nc.sync.dma_start(out=t[:], in_=e_w2[4 * c : 4 * c + 4].rearrange("e a k -> a e k"))
+            rows[("w2", c)] = [t[:, x, :] for x in range(4)]
+
+        load_h(0)
+        load_h(1)
+        load_w1(0, 2)
+        load_h(2)
+        load_h(3)
+        load_w1(1, 1)
+        load_w2(0)
+        load_w1(2, 1)
+        load_w1(3, 1)
+        load_w2(1)
+        for e in range(4, EXPERTS):
+            load_w1(e, 1)
+
+        g8 = keep.tile([P, TILES * EXPERTS], F32, name="g8", tag="g8")
+
+        def gates():
+            g = keep.tile([P, TILES * EXPERTS], F32, name="g", tag="g")
+            nc.scalar.activation(out=g[:], in_=gl[:], func=ACT.Sigmoid)
+            nc.scalar.mul(out=g8[:], in_=g[:], mul=1.0 / EXPERTS)
+
+        tps = {}
+        grps = {}
+        codes = {}
+        scales = {}
+
+        def transposes(job, x):
+            tp = psum.tile([P, 2, 2 * P], F32, name="tp", tag="tp", bufs=3)
+            for r in range(2):
+                words = rows[job][2 * x + r].bitcast(F32)
+                for u in range(2):
+                    nc.tensor.transpose(tp[:, u, r * P : (r + 1) * P], words[:, u::2], ident[:])
+            tps[(job, x)] = tp
+
+        def copy_out(job, x, engine):
+            if x == 0:
+                grp = work.tile([P, 4 * P * 4], BF16, name="grp", tag="grp", bufs=2, align_bytes=64)
+                grps[job] = grp
+            grp_words = grps[job][:].bitcast(F32).rearrange("p (r u) -> p r u", u=2)
+            dst = grp_words[:, x * 2 * P : (x + 1) * 2 * P, :]
+            src = tps[(job, x)][:].rearrange("p u r -> p r u")
+            if engine == "s":
+                nc.scalar.copy(out=dst, in_=src)
+            else:
+                nc.vector.tensor_copy(out=dst, in_=src)
+
+        def quantize_operand(job):
+            c = keep.tile([P, 4 * P], U32, name="c_%s%d" % job, tag="c_%s%d" % job, align_bytes=64)
+            s = keep.tile([P, 4 * P], U8, name="s_%s%d" % job, tag="s_%s%d" % job, align_bytes=64)
+            nc.vector.quantize_mx(out=c[:].bitcast(FP8X4), scales=s[:], in_=grps[job][:])
+            codes[job] = c
+            scales[job] = s
+
+        banks = {}
+        zs = {}
+        zis = {}
+        h1c = {}
+        h1s = {}
+        ps2s = {}
+        ys = {}
+        acc = keep.tile([P, TILES, ACTIONS], F32, name="acc", tag="acc")
+        b2bc = keep.tile([P, EXPERTS, ACTIONS], F32, name="b2bc", tag="b2bc")
+        o0_v = out_0.rearrange("(p i) a -> p i a", i=TILES)
+        o1_v = out_1.rearrange("(p i) e a -> p i e a", i=TILES)
+
+        def first_product(u):
+            e, hf = u // 2, u % 2
+            banks[u] = []
+            for t in range(4):
+                bank = psum.tile([P, HALF * P], BANK_DT, name="bank", tag="bank", bufs=4)
+                nc.tensor.matmul_mx(
+                    out=bank[:],
+                    lhsT=codes[("w1", e)][:, t * P : (t + 1) * P].bitcast(FP8X4),
+                    lhsT_scale=scales[("w1", e)][:, t * P : (t + 1) * P],
+                    rhs=codes[("h", hf)][:].bitcast(FP8X4),
+                    rhs_scale=scales[("h", hf)][:],
+                    start=True,
+                    stop=True,
+                )
+                banks[u].append(bank)
+
+        def scalar_share(u):
+            return S_SHARE if u >= 2 else 0
+
+        def bias_relu(u, engines):
+            e = u // 2
+            z = work.tile([P, 4, HALF * P], BF16, name="z", tag="z", bufs=3)
+            for t in range(4):
+                if engines[t] == "s":
+                    nc.scalar.activation(out=z[:, t, :], in_=banks[u][t][:], func=ACT.Relu, bias=b1[:, e, t : t + 1], scale=1.0)
+                else:
+                    nc.vector.tensor_scalar(out=z[:, t, :], in0=banks[u][t][:], scalar1=b1[:, e, t : t + 1], scalar2=0.0, op0=ALU.add, op1=ALU.max)
+            zs[u] = z
+            zi = work.tile([P, HALF * P, 4], BF16, name="zi", tag="zi", bufs=3, align_bytes=64)
+            zis[u] = zi
+            lo = HALF * P - scalar_share(u)
+            if lo < HALF * P:
+                nc.scalar.copy(out=zi[:, lo:, :], in_=z[:, :, lo:].rearrange("p t n -> p n t"))
+
+        def interleave(u):
+            lo = HALF * P - scalar_share(u)
+            nc.vector.tensor_copy(out=zis[u][:, 0:lo, :], in_=zs[u][:, :, 0:lo].rearrange("p t n -> p n t"))
+
+        def quantize_h1(u):
+            c = work.tile([P, HALF * P], U32, name="h1c", tag="h1c", bufs=3, align_bytes=64)
+            s = work.tile([P, HALF * P], U8, name="h1s", tag="h1s", bufs=3, align_bytes=64)
+            nc.vector.quantize_mx(out=c[:].bitcast(FP8X4), scales=s[:], in_=zis[u][:].rearrange("p n t -> p (n t)"))
+            h1c[u] = c
+            h1s[u] = s
+
+        def second_product(u):
+            e = u // 2
+            w2 = ("w2", e // 4)
+            cols = slice((e % 4) * P, (e % 4 + 1) * P)
+            ps2 = psum.tile([P, HALF, ACTIONS], F32, name="ps2", tag="ps2", bufs=1)
+            for j in range(HALF):
+                nc.tensor.matmul_mx(
+                    out=ps2[:, j, :],
+                    lhsT=h1c[u][:, j * P : (j + 1) * P].bitcast(FP8X4),
+                    lhsT_scale=h1s[u][:, j * P : (j + 1) * P],
+                    rhs=codes[w2][:, cols].bitcast(FP8X4),
+                    rhs_scale=scales[w2][:, cols],
+                    start=True,
+                    stop=True,
+                )
+            ps2s[u] = ps2
+
+        def expert_out(u):
+            e, hf = u // 2, u % 2
+            y = work.tile([P, HALF, ACTIONS], F32, name="y", tag="y", bufs=3)
+            nc.vector.tensor_tensor(out=y[:], in0=ps2s[u][:], in1=b2bc[:, e : e + 1, :].to_broadcast([P, HALF, ACTIONS]), op=ALU.add)
+            nc.sync.dma_start(out=o1_v[:, hf * HALF : (hf + 1) * HALF, e, :], in_=y[:])
+            ys[u] = y
+
+        def gate(u):
+            e, hf = u // 2, u % 2
+            for j in range(HALF):
+                i = hf * HALF + j
+                gcol = g8[:, i * EXPERTS + e : i * EXPERTS + e + 1]
+                if e == 0:
+                    nc.vector.tensor_scalar(out=acc[:, i, :], in0=ys[u][:, j, :], scalar1=gcol, scalar2=None, op0=ALU.mult)
+                else:
+                    nc.vector.scalar_tensor_tensor(out=acc[:, i, :], in0=ys[u][:, j, :], scalar=gcol, in1=acc[:, i, :], op0=ALU.mult, op1=ALU.add)
+
+        def turn(job, engine):
+            for x in range(2):
+                transposes(job, x)
+            if engine == "s":
+                for x in range(2):
+                    copy_out(job, x, "s")
+
+        def spread_b2():
+            for c in range(2):
+                pb = psum.tile([P, 4 * ACTIONS], F32, name="pb", tag="tp", bufs=3)
+                nc.tensor.matmul(out=pb[:], lhsT=ones[:], rhs=b2row[:, c * 4 * ACTIONS : (c + 1) * 4 * ACTIONS], start=True, stop=True)
+                nc.vector.tensor_copy(out=b2bc[:, 4 * c : 4 * c + 4, :].rearrange("p e a -> p (e a)"), in_=pb[:])
+
+        transposes(("h", 0), 0)
+        copy_out(("h", 0), 0, "s")
+        transposes(("h", 0), 1)
+        copy_out(("h", 0), 1, "v")
+        transposes(("w1", 0), 0)
+        copy_out(("w1", 0), 0, "s")
+        quantize_operand(("h", 0))
+        transposes(("w1", 0), 1)
+        copy_out(("w1", 0), 1, "v")
+        turn(("h", 1), "s")
+        quantize_operand(("w1", 0))
+        first_product(0)
+        quantize_operand(("h", 1))
+        bias_relu(0, "ssvv")
+        turn(("w1", 1), "s")
+        first_product(1)
+        bias_relu(1, "ssss")
+        gates()
+
+        turn_at = {
+            -1: (("w1", 1), "s"),
+            0: (("w2", 0), "v"),
+            1: (("w1", 2), "s"),
+            3: (("w1", 3), "s"),
+            4: (("w2", 1), "s"),
+            5: (("w1", 4), "s"),
+            7: (("w1", 5), "s"),
+            9: (("w1", 6), "s"),
+            11: (("w1", 7), "s"),
+        }
+        for k in range(UNITS + 1):
+            if 1 <= k < UNITS - 1:
+                first_product(k + 1)
+                bias_relu(k + 1, "ssss")
+            if k in turn_at:
+                turn(turn_at[k][0], turn_at[k][1])
+            if k < UNITS:
+                interleave(k)
+            if k - 1 in turn_at:
+                quantize_operand(turn_at[k - 1][0])
+            if k >= 2:
+                expert_out(k - 2)
+            if k < UNITS:
+                quantize_h1(k)
+            if k in turn_at and turn_at[k][1] == "v":
+                for x in range(2):
+                    copy_out(turn_at[k][0], x, "v")
+            if k == 1:
+                spread_b2()
+            if k >= 2:
+                gate(k - 2)
+            if k >= 1:
+                second_product(k - 1)
+        nc.sync.dma_start(out=o0_v[:, 0:HALF, :], in_=acc[:, 0:HALF, :])
+        expert_out(UNITS - 1)
+        gate(UNITS - 1)
+        nc.sync.dma_start(out=o0_v[:, HALF:TILES, :], in_=acc[:, HALF:TILES, :])

@@ -31,7 +31,6 @@ def tile_mspagent_pb_kernel(tc, h, gate_logit, e_w1, e_b1, e_w2, e_b2, out_0, ou
         keep = ctx.enter_context(tc.tile_pool(name="keep", bufs=1))
         work = ctx.enter_context(tc.tile_pool(name="work", bufs=2))
         psum = ctx.enter_context(tc.psum_pool(name="psum", bufs=2))
-        ctx.enter_context(tc.manual_schedule())
 
         warm = keep.tile([P, 1], F32, name="warm", tag="warm")
         nc.gpsimd.memset(warm[:], 0.0)
@@ -138,7 +137,7 @@ def tile_mspagent_pb_kernel(tc, h, gate_logit, e_w1, e_b1, e_w2, e_b2, out_0, ou
             e, hf = u // 2, u % 2
             banks[u] = []
             for t in range(4):
-                bank = psum.tile([P, HALF * P], BANK_DT, name="bank", tag="bank", bufs=4)
+                bank = psum.tile([P, HALF * P], BANK_DT, name="bank", tag="bank", bufs=3)
                 nc.tensor.matmul_mx(
                     out=bank[:],
                     lhsT=codes[("w1", e)][:, t * P : (t + 1) * P].bitcast(FP8X4),
@@ -183,7 +182,7 @@ def tile_mspagent_pb_kernel(tc, h, gate_logit, e_w1, e_b1, e_w2, e_b2, out_0, ou
             e = u // 2
             w2 = ("w2", e // 4)
             cols = slice((e % 4) * P, (e % 4 + 1) * P)
-            ps2 = psum.tile([P, HALF, ACTIONS], F32, name="ps2", tag="ps2", bufs=1)
+            ps2 = psum.tile([P, HALF, ACTIONS], F32, name="ps2", tag="ps2", bufs=2)
             for j in range(HALF):
                 nc.tensor.matmul_mx(
                     out=ps2[:, j, :],

@@ -36,17 +36,12 @@ def tile_mspagent_pb_kernel(tc, h, gate_logit, e_w1, e_b1, e_w2, e_b2, out_0, ou
         nc.gpsimd.memset(warm[:], 0.0)
         ident = keep.tile([P, P], F32, name="ident", tag="ident")
         make_identity(nc, ident[:])
-        b2row = keep.tile([P, EXPERTS * ACTIONS], BF16, name="b2row", tag="b2row")
-        nc.gpsimd.memset(b2row[:], 0.0)
-        ones = keep.tile([P, P], BF16, name="ones", tag="ones")
-        nc.gpsimd.memset(ones[:], 1.0)
 
         b1 = keep.tile([P, EXPERTS, 4], BF16, name="b1", tag="b1")
         nc.scalar.dma_start(out=b1[:], in_=e_b1.rearrange("e (m t) -> m e t", t=4))
         gl = keep.tile([P, TILES * EXPERTS], BF16, name="gl", tag="gl")
         nc.scalar.dma_start(out=gl[:], in_=gate_logit.rearrange("(p i) e -> p (i e)", i=TILES))
         nc.scalar.activation(out=warm[:], in_=warm[:], func=ACT.Sigmoid)
-        nc.scalar.dma_start(out=b2row[0:1, :], in_=e_b2.rearrange("(o e) a -> o (e a)", o=1))
 
         h_v = h.rearrange("(p i) k -> p i k", i=TILES)
         rows = {}
@@ -77,6 +72,8 @@ def tile_mspagent_pb_kernel(tc, h, gate_logit, e_w1, e_b1, e_w2, e_b2, out_0, ou
         load_w1(1, 1)
         load_w2(0)
         load_w1(2, 1)
+        b2bc = keep.tile([P, EXPERTS, ACTIONS], BF16, name="b2bc", tag="b2bc")
+        nc.sync.dma_start(out=b2bc[:].rearrange("p e a -> p (e a)"), in_=e_b2.rearrange("e a -> (e a)").partition_broadcast(P))
         load_w1(3, 1)
         load_w2(1)
         for e in range(4, EXPERTS):
@@ -129,7 +126,6 @@ def tile_mspagent_pb_kernel(tc, h, gate_logit, e_w1, e_b1, e_w2, e_b2, out_0, ou
         ps2s = {}
         ys = {}
         acc = keep.tile([P, TILES, ACTIONS], F32, name="acc", tag="acc")
-        b2bc = keep.tile([P, EXPERTS, ACTIONS], F32, name="b2bc", tag="b2bc")
         o0_v = out_0.rearrange("(p i) a -> p i a", i=TILES)
         o1_v = out_1.rearrange("(p i) e a -> p i e a", i=TILES)
 
@@ -165,11 +161,11 @@ def tile_mspagent_pb_kernel(tc, h, gate_logit, e_w1, e_b1, e_w2, e_b2, out_0, ou
             zis[u] = zi
             lo = HALF * P - scalar_share(u)
             if lo < HALF * P:
-                nc.scalar.copy(out=zi[:, lo:, :], in_=z[:, :, lo:].rearrange("p t n -> p n t"))
+                nc.scalar.copy(out=zi[:, lo:, :].rearrange("p (c i) t -> p c t i", i=4), in_=z[:, :, lo:].rearrange("p t (c i) -> p c t i", i=4))
 
         def interleave(u):
             lo = HALF * P - scalar_share(u)
-            nc.vector.tensor_copy(out=zis[u][:, 0:lo, :], in_=zs[u][:, :, 0:lo].rearrange("p t n -> p n t"))
+            nc.vector.tensor_copy(out=zis[u][:, 0:lo, :].rearrange("p (c i) t -> p c t i", i=4), in_=zs[u][:, :, 0:lo].rearrange("p t (c i) -> p c t i", i=4))
 
         def quantize_h1(u):
             c = work.tile([P, HALF * P], U32, name="h1c", tag="h1c", bufs=3, align_bytes=64)
@@ -219,12 +215,6 @@ def tile_mspagent_pb_kernel(tc, h, gate_logit, e_w1, e_b1, e_w2, e_b2, out_0, ou
                 for x in range(2):
                     copy_out(job, x, "s")
 
-        def spread_b2():
-            for c in range(2):
-                pb = psum.tile([P, 4 * ACTIONS], F32, name="pb", tag="tp", bufs=3)
-                nc.tensor.matmul(out=pb[:], lhsT=ones[:], rhs=b2row[:, c * 4 * ACTIONS : (c + 1) * 4 * ACTIONS], start=True, stop=True)
-                nc.vector.tensor_copy(out=b2bc[:, 4 * c : 4 * c + 4, :].rearrange("p e a -> p (e a)"), in_=pb[:])
-
         transposes(("h", 0), 0)
         copy_out(("h", 0), 0, "s")
         transposes(("h", 0), 1)
@@ -272,8 +262,6 @@ def tile_mspagent_pb_kernel(tc, h, gate_logit, e_w1, e_b1, e_w2, e_b2, out_0, ou
             if k in turn_at and turn_at[k][1] == "v":
                 for x in range(2):
                     copy_out(turn_at[k][0], x, "v")
-            if k == 1:
-                spread_b2()
             if k >= 2:
                 gate(k - 2)
             if k >= 1:

@@ -21,6 +21,8 @@ HALF = 4
 UNITS = 2 * EXPERTS
 BANK_DT = BF16
 S_SHARE = 64
+LATE_S = {14: 128, 15: 320}
+WARM_FIRST = 3
 
 FLOPS = 2 * TOKENS * HID * HID * EXPERTS + 2 * TOKENS * HID * ACTIONS * EXPERTS
 
@@ -32,6 +34,13 @@ def tile_mspagent_pb_kernel(tc, h, gate_logit, e_w1, e_b1, e_w2, e_b2, out_0, ou
         work = ctx.enter_context(tc.tile_pool(name="work", bufs=2))
         psum = ctx.enter_context(tc.psum_pool(name="psum", bufs=2))
 
+        wl = keep.tile([P, P], BF16, name="wl", tag="wl")
+        nc.gpsimd.memset(wl[:], 0.0)
+        wr = keep.tile([P, HALF * P], BF16, name="wr", tag="wr")
+        nc.gpsimd.memset(wr[:], 0.0)
+        pd = psum.tile([P, HALF * P], F32, name="pd", tag="ps2", bufs=2)
+        for x in range(WARM_FIRST):
+            nc.tensor.matmul(out=pd[:], lhsT=wl[:], rhs=wr[:], start=True, stop=True)
         warm = keep.tile([P, 1], F32, name="warm", tag="warm")
         nc.gpsimd.memset(warm[:], 0.0)
         ident = keep.tile([P, P], F32, name="ident", tag="ident")
@@ -146,7 +155,7 @@ def tile_mspagent_pb_kernel(tc, h, gate_logit, e_w1, e_b1, e_w2, e_b2, out_0, ou
                 banks[u].append(bank)
 
         def scalar_share(u):
-            return S_SHARE if u >= 2 else 0
+            return LATE_S.get(u, S_SHARE) if u >= 2 else 0
 
         def bias_relu(u, engines):
             e = u // 2
@@ -165,7 +174,7 @@ def tile_mspagent_pb_kernel(tc, h, gate_logit, e_w1, e_b1, e_w2, e_b2, out_0, ou
 
         def interleave(u):
             lo = HALF * P - scalar_share(u)
-            nc.vector.tensor_copy(out=zis[u][:, 0:lo, :].rearrange("p (c i) t -> p c t i", i=4), in_=zs[u][:, :, 0:lo].rearrange("p t (c i) -> p c t i", i=4))
+            nc.vector.tensor_copy(out=zis[u][:, 0:lo, :].rearrange("p (c h i) t -> p h c t i", h=2, i=4), in_=zs[u][:, :, 0:lo].rearrange("p t (c h i) -> p h c t i", h=2, i=4))
 
         def quantize_h1(u):
             c = work.tile([P, HALF * P], U32, name="h1c", tag="h1c", bufs=3, align_bytes=64)

@@ -23,6 +23,7 @@ BANK_DT = BF16
 S_SHARE = 64
 LATE_S = {14: 128, 15: 320}
 WARM_FIRST = 3
+RUN = 8
 
 FLOPS = 2 * TOKENS * HID * HID * EXPERTS + 2 * TOKENS * HID * ACTIONS * EXPERTS
 
@@ -170,11 +171,11 @@ def tile_mspagent_pb_kernel(tc, h, gate_logit, e_w1, e_b1, e_w2, e_b2, out_0, ou
             zis[u] = zi
             lo = HALF * P - scalar_share(u)
             if lo < HALF * P:
-                nc.scalar.copy(out=zi[:, lo:, :].rearrange("p (c i) t -> p c t i", i=4), in_=z[:, :, lo:].rearrange("p t (c i) -> p c t i", i=4))
+                nc.scalar.copy(out=zi[:, lo:, :].rearrange("p (c i) t -> p c t i", i=RUN), in_=z[:, :, lo:].rearrange("p t (c i) -> p c t i", i=RUN))
 
         def interleave(u):
             lo = HALF * P - scalar_share(u)
-            nc.vector.tensor_copy(out=zis[u][:, 0:lo, :].rearrange("p (c h i) t -> p h c t i", h=2, i=4), in_=zs[u][:, :, 0:lo].rearrange("p t (c h i) -> p h c t i", h=2, i=4))
+            nc.vector.tensor_copy(out=zis[u][:, 0:lo, :].rearrange("p (c h i) t -> p h c t i", h=2, i=RUN), in_=zs[u][:, :, 0:lo].rearrange("p t (c h i) -> p h c t i", h=2, i=RUN))
 
         def quantize_h1(u):
             c = work.tile([P, HALF * P], U32, name="h1c", tag="h1c", bufs=3, align_bytes=64)

@@ -111,7 +111,7 @@ def tile_mspagent_pb_kernel(tc, h, gate_logit, e_w1, e_b1, e_w2, e_b2, out_0, ou
 
         def copy_out(job, x, engine):
             if x == 0:
-                grp = work.tile([P, 4 * P * 4], BF16, name="grp", tag="grp", bufs=2, align_bytes=64)
+                grp = work.tile([P, 4 * P * 4], BF16, name="grp", tag="grp", bufs=3, align_bytes=64)
                 grps[job] = grp
             grp_words = grps[job][:].bitcast(F32).rearrange("p (r u) -> p r u", u=2)
             dst = grp_words[:, x * 2 * P : (x + 1) * 2 * P, :]
@@ -244,38 +244,61 @@ def tile_mspagent_pb_kernel(tc, h, gate_logit, e_w1, e_b1, e_w2, e_b2, out_0, ou
         bias_relu(1, "ssss")
         gates()
 
-        turn_at = {
-            -1: (("w1", 1), "s"),
-            0: (("w2", 0), "v"),
-            1: (("w1", 2), "s"),
-            3: (("w1", 3), "s"),
-            4: (("w2", 1), "s"),
-            5: (("w1", 4), "s"),
-            7: (("w1", 5), "s"),
-            9: (("w1", 6), "s"),
-            11: (("w1", 7), "s"),
+        early_at = {
+            0: [(("w2", 0), 0, "v"), (("w2", 0), 1, "v")],
+            1: [(("w1", 2), 0, "s"), (("w1", 2), 1, "s")],
+            2: [(("w1", 3), 0, "s")],
+            3: [(("w1", 3), 1, "s")],
+            4: [(("w1", 4), 0, "s")],
+            5: [(("w1", 4), 1, "s")],
+            6: [(("w1", 5), 0, "s")],
+            7: [(("w1", 5), 1, "s")],
+            8: [(("w1", 6), 0, "s")],
+            9: [(("w1", 6), 1, "s")],
+            10: [(("w1", 7), 0, "s")],
+            11: [(("w1", 7), 1, "s")],
         }
+        late_at = {2: [(("w2", 1), 0, "s")], 4: [(("w2", 1), 1, "s")]}
+        quant_at = {
+            0: [("w1", 1)],
+            1: [("w2", 0)],
+            2: [("w1", 2)],
+            4: [("w1", 3)],
+            5: [("w2", 1)],
+            6: [("w1", 4)],
+            8: [("w1", 5)],
+            10: [("w1", 6)],
+            12: [("w1", 7)],
+        }
+
+        def half_jobs(jobs):
+            for job, x, engine in jobs:
+                transposes(job, x)
+            for job, x, engine in jobs:
+                if engine == "s":
+                    copy_out(job, x, "s")
+
         for k in range(UNITS + 1):
             if 1 <= k < UNITS - 1:
                 first_product(k + 1)
                 bias_relu(k + 1, "ssss")
-            if k in turn_at:
-                turn(turn_at[k][0], turn_at[k][1])
+            half_jobs(early_at.get(k, []))
             if k < UNITS:
                 interleave(k)
-            if k - 1 in turn_at:
-                quantize_operand(turn_at[k - 1][0])
+            for job in quant_at.get(k, []):
+                quantize_operand(job)
             if k >= 2:
                 expert_out(k - 2)
             if k < UNITS:
                 quantize_h1(k)
-            if k in turn_at and turn_at[k][1] == "v":
-                for x in range(2):
-                    copy_out(turn_at[k][0], x, "v")
+            for job, x, engine in early_at.get(k, []):
+                if engine == "v":
+                    copy_out(job, x, "v")
             if k >= 2:
                 gate(k - 2)
             if k >= 1:
                 second_product(k - 1)
+            half_jobs(late_at.get(k, []))
         nc.sync.dma_start(out=o0_v[:, 0:HALF, :], in_=acc[:, 0:HALF, :])
         expert_out(UNITS - 1)
         gate(UNITS - 1)

@@ -47,8 +47,16 @@ def tile_mspagent_pb_kernel(tc, h, gate_logit, e_w1, e_b1, e_w2, e_b2, out_0, ou
         ident = keep.tile([P, P], F32, name="ident", tag="ident")
         make_identity(nc, ident[:])
 
-        b1 = keep.tile([P, EXPERTS, 4], BF16, name="b1", tag="b1")
-        nc.scalar.dma_start(out=b1[:], in_=e_b1.rearrange("e (m t) -> m e t", t=4))
+        b1_view = e_b1.rearrange("e (m t) -> m e t", t=4)
+        b1_first = keep.tile([P, 1, 4], BF16, name="b1_first", tag="b1_first")
+        nc.scalar.dma_start(out=b1_first[:], in_=b1_view[:, 0:1, :])
+        b1_rest = keep.tile([P, EXPERTS - 1, 4], BF16, name="b1_rest", tag="b1_rest")
+
+        def b1_col(e, t):
+            if e == 0:
+                return b1_first[:, 0, t : t + 1]
+            return b1_rest[:, e - 1, t : t + 1]
+
         gl = keep.tile([P, TILES * EXPERTS], BF16, name="gl", tag="gl")
         nc.scalar.dma_start(out=gl[:], in_=gate_logit.rearrange("(p i) e -> p (i e)", i=TILES))
         nc.scalar.activation(out=warm[:], in_=warm[:], func=ACT.Sigmoid)
@@ -80,6 +88,7 @@ def tile_mspagent_pb_kernel(tc, h, gate_logit, e_w1, e_b1, e_w2, e_b2, out_0, ou
         load_h(2)
         load_h(3)
         load_w1(1, 1)
+        nc.sync.dma_start(out=b1_rest[:], in_=b1_view[:, 1:EXPERTS, :])
         load_w2(0)
         load_w1(2, 1)
         b2bc = keep.tile([P, EXPERTS, ACTIONS], BF16, name="b2bc", tag="b2bc")
@@ -128,6 +137,15 @@ def tile_mspagent_pb_kernel(tc, h, gate_logit, e_w1, e_b1, e_w2, e_b2, out_0, ou
             codes[job] = c
             scales[job] = s
 
+        def quantize_half(job, x):
+            if x == 0:
+                c = keep.tile([P, 4 * P], U32, name="c_%s%d" % job, tag="c_%s%d" % job, align_bytes=64)
+                s = keep.tile([P, 4 * P], U8, name="s_%s%d" % job, tag="s_%s%d" % job, align_bytes=64)
+                codes[job] = c
+                scales[job] = s
+            cols = slice(x * 2 * P, (x + 1) * 2 * P)
+            nc.vector.quantize_mx(out=codes[job][:, cols].bitcast(FP8X4), scales=scales[job][:, cols], in_=grps[job][:, x * 8 * P : (x + 1) * 8 * P])
+
         banks = {}
         zs = {}
         zis = {}
@@ -163,9 +181,9 @@ def tile_mspagent_pb_kernel(tc, h, gate_logit, e_w1, e_b1, e_w2, e_b2, out_0, ou
             z = work.tile([P, 4, HALF * P], BF16, name="z", tag="z", bufs=3)
             for t in range(4):
                 if engines[t] == "s":
-                    nc.scalar.activation(out=z[:, t, :], in_=banks[u][t][:], func=ACT.Relu, bias=b1[:, e, t : t + 1], scale=1.0)
+                    nc.scalar.activation(out=z[:, t, :], in_=banks[u][t][:], func=ACT.Relu, bias=b1_col(e, t), scale=1.0)
                 else:
-                    nc.vector.tensor_scalar(out=z[:, t, :], in0=banks[u][t][:], scalar1=b1[:, e, t : t + 1], scalar2=0.0, op0=ALU.add, op1=ALU.max)
+                    nc.vector.tensor_scalar(out=z[:, t, :], in0=banks[u][t][:], scalar1=b1_col(e, t), scalar2=0.0, op0=ALU.add, op1=ALU.max)
             zs[u] = z
             zi = work.tile([P, HALF * P, 4], BF16, name="zi", tag="zi", bufs=3, align_bytes=64)
             zis[u] = zi
@@ -178,8 +196,8 @@ def tile_mspagent_pb_kernel(tc, h, gate_logit, e_w1, e_b1, e_w2, e_b2, out_0, ou
             nc.vector.tensor_copy(out=zis[u][:, 0:lo, :].rearrange("p (c h i) t -> p h c t i", h=2, i=RUN), in_=zs[u][:, :, 0:lo].rearrange("p t (c h i) -> p h c t i", h=2, i=RUN))
 
         def quantize_h1(u):
-            c = work.tile([P, HALF * P], U32, name="h1c", tag="h1c", bufs=3, align_bytes=64)
-            s = work.tile([P, HALF * P], U8, name="h1s", tag="h1s", bufs=3, align_bytes=64)
+            c = work.tile([P, HALF * P], U32, name="h1c", tag="h1c", bufs=UNITS, align_bytes=64)
+            s = work.tile([P, HALF * P], U8, name="h1s", tag="h1s", bufs=UNITS, align_bytes=64)
             nc.vector.quantize_mx(out=c[:].bitcast(FP8X4), scales=s[:], in_=zis[u][:].rearrange("p n t -> p (n t)"))
             h1c[u] = c
             h1s[u] = s
@@ -203,7 +221,7 @@ def tile_mspagent_pb_kernel(tc, h, gate_logit, e_w1, e_b1, e_w2, e_b2, out_0, ou
 
         def expert_out(u):
             e, hf = u // 2, u % 2
-            y = work.tile([P, HALF, ACTIONS], F32, name="y", tag="y", bufs=3)
+            y = work.tile([P, HALF, ACTIONS], F32, name="y", tag="y", bufs=UNITS)
             nc.vector.tensor_tensor(out=y[:], in0=ps2s[u][:], in1=b2bc[:, e : e + 1, :].to_broadcast([P, HALF, ACTIONS]), op=ALU.add)
             nc.sync.dma_start(out=o1_v[:, hf * HALF : (hf + 1) * HALF, e, :], in_=y[:])
             ys[u] = y
@@ -232,10 +250,11 @@ def tile_mspagent_pb_kernel(tc, h, gate_logit, e_w1, e_b1, e_w2, e_b2, out_0, ou
         transposes(("w1", 0), 0)
         copy_out(("w1", 0), 0, "s")
         quantize_operand(("h", 0))
+        quantize_half(("w1", 0), 0)
         transposes(("w1", 0), 1)
         copy_out(("w1", 0), 1, "v")
         turn(("h", 1), "s")
-        quantize_operand(("w1", 0))
+        quantize_half(("w1", 0), 1)
         first_product(0)
         quantize_operand(("h", 1))
         bias_relu(0, "ssvv")

@@ -50,12 +50,14 @@ def tile_mspagent_pb_kernel(tc, h, gate_logit, e_w1, e_b1, e_w2, e_b2, out_0, ou
         b1_view = e_b1.rearrange("e (m t) -> m e t", t=4)
         b1_first = keep.tile([P, 1, 4], BF16, name="b1_first", tag="b1_first")
         nc.scalar.dma_start(out=b1_first[:], in_=b1_view[:, 0:1, :])
-        b1_rest = keep.tile([P, EXPERTS - 1, 4], BF16, name="b1_rest", tag="b1_rest")
+        b1_rows = keep.tile([P, HID], BF16, name="b1_rows", tag="b1_rows")
+        nc.vector.memset(b1_rows[:], 0.0)
+        b1_all = keep.tile([P, EXPERTS, 4], BF16, name="b1_all", tag="b1_all")
 
         def b1_col(e, t):
             if e == 0:
                 return b1_first[:, 0, t : t + 1]
-            return b1_rest[:, e - 1, t : t + 1]
+            return b1_all[:, e, t : t + 1]
 
         gl = keep.tile([P, TILES * EXPERTS], BF16, name="gl", tag="gl")
         nc.scalar.dma_start(out=gl[:], in_=gate_logit.rearrange("(p i) e -> p (i e)", i=TILES))
@@ -87,8 +89,8 @@ def tile_mspagent_pb_kernel(tc, h, gate_logit, e_w1, e_b1, e_w2, e_b2, out_0, ou
         load_w1(0, 2)
         load_h(2)
         load_h(3)
+        nc.sync.dma_start(out=b1_rows[0:EXPERTS, :], in_=e_b1)
         load_w1(1, 1)
-        nc.sync.dma_start(out=b1_rest[:], in_=b1_view[:, 1:EXPERTS, :])
         load_w2(0)
         load_w1(2, 1)
         b2bc = keep.tile([P, EXPERTS, ACTIONS], BF16, name="b2bc", tag="b2bc")
@@ -129,6 +131,14 @@ def tile_mspagent_pb_kernel(tc, h, gate_logit, e_w1, e_b1, e_w2, e_b2, out_0, ou
                 nc.scalar.copy(out=dst, in_=src)
             else:
                 nc.vector.tensor_copy(out=dst, in_=src)
+
+        def turn_bias():
+            tb = psum.tile([P, 2, P], F32, name="tb", tag="tp", bufs=3)
+            words = b1_rows[:].bitcast(F32)
+            for u in range(2):
+                nc.tensor.transpose(tb[:, u, :], words[:, u::2], ident[:])
+            b1_words = b1_all[:].rearrange("p e t -> p (e t)").bitcast(F32).rearrange("p (e u) -> p e u", u=2)
+            nc.vector.tensor_copy(out=b1_words, in_=tb[:, :, 0:EXPERTS].rearrange("p u e -> p e u"))
 
         def quantize_operand(job):
             c = keep.tile([P, 4 * P], U32, name="c_%s%d" % job, tag="c_%s%d" % job, align_bytes=64)
@@ -302,6 +312,8 @@ def tile_mspagent_pb_kernel(tc, h, gate_logit, e_w1, e_b1, e_w2, e_b2, out_0, ou
                 first_product(k + 1)
                 bias_relu(k + 1, "ssss")
             half_jobs(early_at.get(k, []))
+            if k == 0:
+                turn_bias()
             if k < UNITS:
                 interleave(k)
             for job in quant_at.get(k, []):

@@ -330,7 +330,7 @@ def tile_mspagent_pb_kernel(tc, h, gate_logit, e_w1, e_b1, e_w2, e_b2, out_0, ou
             if k >= 1:
                 second_product(k - 1)
             half_jobs(late_at.get(k, []))
-        nc.sync.dma_start(out=o0_v[:, 0:HALF, :], in_=acc[:, 0:HALF, :])
+        nc.scalar.dma_start(out=o0_v[:, 0:HALF, :], in_=acc[:, 0:HALF, :])
         expert_out(UNITS - 1)
         gate(UNITS - 1)
-        nc.sync.dma_start(out=o0_v[:, HALF:TILES, :], in_=acc[:, HALF:TILES, :])
+        nc.scalar.dma_start(out=o0_v[:, HALF:TILES, :], in_=acc[:, HALF:TILES, :])

@@ -122,7 +122,7 @@ def tile_mspagent_pb_kernel(tc, h, gate_logit, e_w1, e_b1, e_w2, e_b2, out_0, ou
 
         def copy_out(job, x, engine):
             if x == 0:
-                grp = work.tile([P, 4 * P * 4], BF16, name="grp", tag="grp", bufs=3, align_bytes=64)
+                grp = work.tile([P, 4 * P * 4], BF16, name="grp", tag="grp", bufs=3, align_bytes=256)
                 grps[job] = grp
             grp_words = grps[job][:].bitcast(F32).rearrange("p (r u) -> p r u", u=2)
             dst = grp_words[:, x * 2 * P : (x + 1) * 2 * P, :]
@@ -141,16 +141,16 @@ def tile_mspagent_pb_kernel(tc, h, gate_logit, e_w1, e_b1, e_w2, e_b2, out_0, ou
             nc.vector.tensor_copy(out=b1_words, in_=tb[:, :, 0:EXPERTS].rearrange("p u e -> p e u"))
 
         def quantize_operand(job):
-            c = keep.tile([P, 4 * P], U32, name="c_%s%d" % job, tag="c_%s%d" % job, align_bytes=64)
-            s = keep.tile([P, 4 * P], U8, name="s_%s%d" % job, tag="s_%s%d" % job, align_bytes=64)
+            c = keep.tile([P, 4 * P], U32, name="c_%s%d" % job, tag="c_%s%d" % job, align_bytes=256)
+            s = keep.tile([P, 4 * P], U8, name="s_%s%d" % job, tag="s_%s%d" % job, align_bytes=256)
             nc.vector.quantize_mx(out=c[:].bitcast(FP8X4), scales=s[:], in_=grps[job][:])
             codes[job] = c
             scales[job] = s
 
         def quantize_half(job, x):
             if x == 0:
-                c = keep.tile([P, 4 * P], U32, name="c_%s%d" % job, tag="c_%s%d" % job, align_bytes=64)
-                s = keep.tile([P, 4 * P], U8, name="s_%s%d" % job, tag="s_%s%d" % job, align_bytes=64)
+                c = keep.tile([P, 4 * P], U32, name="c_%s%d" % job, tag="c_%s%d" % job, align_bytes=256)
+                s = keep.tile([P, 4 * P], U8, name="s_%s%d" % job, tag="s_%s%d" % job, align_bytes=256)
                 codes[job] = c
                 scales[job] = s
             cols = slice(x * 2 * P, (x + 1) * 2 * P)
@@ -195,7 +195,7 @@ def tile_mspagent_pb_kernel(tc, h, gate_logit, e_w1, e_b1, e_w2, e_b2, out_0, ou
                 else:
                     nc.vector.tensor_scalar(out=z[:, t, :], in0=banks[u][t][:], scalar1=b1_col(e, t), scalar2=0.0, op0=ALU.add, op1=ALU.max)
             zs[u] = z
-            zi = work.tile([P, HALF * P, 4], BF16, name="zi", tag="zi", bufs=3, align_bytes=64)
+            zi = work.tile([P, HALF * P, 4], BF16, name="zi", tag="zi", bufs=3, align_bytes=256)
             zis[u] = zi
             lo = HALF * P - scalar_share(u)
             if lo < HALF * P:
@@ -206,8 +206,8 @@ def tile_mspagent_pb_kernel(tc, h, gate_logit, e_w1, e_b1, e_w2, e_b2, out_0, ou
             nc.vector.tensor_copy(out=zis[u][:, 0:lo, :].rearrange("p (c h i) t -> p h c t i", h=2, i=RUN), in_=zs[u][:, :, 0:lo].rearrange("p t (c h i) -> p h c t i", h=2, i=RUN))
 
         def quantize_h1(u):
-            c = work.tile([P, HALF * P], U32, name="h1c", tag="h1c", bufs=UNITS, align_bytes=64)
-            s = work.tile([P, HALF * P], U8, name="h1s", tag="h1s", bufs=UNITS, align_bytes=64)
+            c = work.tile([P, HALF * P], U32, name="h1c", tag="h1c", bufs=UNITS, align_bytes=256)
+            s = work.tile([P, HALF * P], U8, name="h1s", tag="h1s", bufs=UNITS, align_bytes=256)
             nc.vector.quantize_mx(out=c[:].bitcast(FP8X4), scales=s[:], in_=zis[u][:].rearrange("p n t -> p (n t)"))
             h1c[u] = c
             h1s[u] = s

from contextlib import ExitStack

import concourse.mybir as mybir
from concourse.masks import make_identity

F32 = mybir.dt.float32
BF16 = mybir.dt.bfloat16
U32 = mybir.dt.uint32
U8 = mybir.dt.uint8
FP8X4 = mybir.dt.float8_e4m3fn_x4
ACT = mybir.ActivationFunctionType
ALU = mybir.AluOpType

P = 128
TOKENS = 1024
HID = 512
EXPERTS = 8
ACTIONS = 128
TILES = TOKENS // P
HALF = 4
UNITS = 2 * EXPERTS
BANK_DT = BF16
S_SHARE = 64
LATE_S = {14: 128, 15: 320}
WARM_FIRST = 3
RUN = 8

FLOPS = 2 * TOKENS * HID * HID * EXPERTS + 2 * TOKENS * HID * ACTIONS * EXPERTS


def tile_mspagent_pb_kernel(tc, h, gate_logit, e_w1, e_b1, e_w2, e_b2, out_0, out_1):
    nc = tc.nc
    with ExitStack() as ctx:
        keep = ctx.enter_context(tc.tile_pool(name="keep", bufs=1))
        work = ctx.enter_context(tc.tile_pool(name="work", bufs=2))
        psum = ctx.enter_context(tc.psum_pool(name="psum", bufs=2))

        wl = keep.tile([P, P], BF16, name="wl", tag="wl")
        nc.gpsimd.memset(wl[:], 0.0)
        wr = keep.tile([P, HALF * P], BF16, name="wr", tag="wr")
        nc.gpsimd.memset(wr[:], 0.0)
        pd = psum.tile([P, HALF * P], F32, name="pd", tag="ps2", bufs=2)
        for x in range(WARM_FIRST):
            nc.tensor.matmul(out=pd[:], lhsT=wl[:], rhs=wr[:], start=True, stop=True)
        warm = keep.tile([P, 1], F32, name="warm", tag="warm")
        nc.gpsimd.memset(warm[:], 0.0)
        ident = keep.tile([P, P], F32, name="ident", tag="ident")
        make_identity(nc, ident[:])

        b1_view = e_b1.rearrange("e (m t) -> m e t", t=4)
        b1_first = keep.tile([P, 1, 4], BF16, name="b1_first", tag="b1_first")
        nc.scalar.dma_start(out=b1_first[:], in_=b1_view[:, 0:1, :])
        b1_rows = keep.tile([P, HID], BF16, name="b1_rows", tag="b1_rows")
        nc.vector.memset(b1_rows[:], 0.0)
        b1_all = keep.tile([P, EXPERTS, 4], BF16, name="b1_all", tag="b1_all")

        def b1_col(e, t):
            if e == 0:
                return b1_first[:, 0, t : t + 1]
            return b1_all[:, e, t : t + 1]

        gl = keep.tile([P, TILES * EXPERTS], BF16, name="gl", tag="gl")
        nc.scalar.dma_start(out=gl[:], in_=gate_logit.rearrange("(p i) e -> p (i e)", i=TILES))
        nc.scalar.activation(out=warm[:], in_=warm[:], func=ACT.Sigmoid)

        h_v = h.rearrange("(p i) k -> p i k", i=TILES)
        rows = {}

        def load_h(c):
            t = keep.tile([P, 2, HID], BF16, name="h_sb%d" % c, tag="h_sb%d" % c)
            nc.sync.dma_start(out=t[:], in_=h_v[:, 2 * c : 2 * c + 2, :])
            rows.setdefault(("h", c // 2), []).extend([t[:, 0, :], t[:, 1, :]])

        def load_w1(e, pieces):
            w1_v = e_w1[e].rearrange("(m t) k -> m t k", t=4)
            n = 4 // pieces
            for c in range(pieces):
                t = keep.tile([P, n, HID], BF16, name="w1_sb%d_%d" % (e, c), tag="w1_sb%d_%d" % (e, c))
                nc.sync.dma_start(out=t[:], in_=w1_v[:, c * n : (c + 1) * n, :])
                rows.setdefault(("w1", e), []).extend([t[:, x, :] for x in range(n)])

        def load_w2(c):
            t = keep.tile([P, 4, HID], BF16, name="w2_sb%d" % c, tag="w2_sb%d" % c)
            nc.sync.dma_start(out=t[:], in_=e_w2[4 * c : 4 * c + 4].rearrange("e a k -> a e k"))
            rows[("w2", c)] = [t[:, x, :] for x in range(4)]

        load_h(0)
        load_h(1)
        load_w1(0, 2)
        load_h(2)
        load_h(3)
        nc.sync.dma_start(out=b1_rows[0:EXPERTS, :], in_=e_b1)
        load_w1(1, 1)
        load_w2(0)
        load_w1(2, 1)
        b2bc = keep.tile([P, EXPERTS, ACTIONS], BF16, name="b2bc", tag="b2bc")
        nc.sync.dma_start(out=b2bc[:].rearrange("p e a -> p (e a)"), in_=e_b2.rearrange("e a -> (e a)").partition_broadcast(P))
        load_w1(3, 1)
        load_w2(1)
        for e in range(4, EXPERTS):
            load_w1(e, 1)

        g8 = keep.tile([P, TILES * EXPERTS], F32, name="g8", tag="g8")

        def gates():
            g = keep.tile([P, TILES * EXPERTS], F32, name="g", tag="g")
            nc.scalar.activation(out=g[:], in_=gl[:], func=ACT.Sigmoid)
            nc.scalar.mul(out=g8[:], in_=g[:], mul=1.0 / EXPERTS)

        tps = {}
        grps = {}
        codes = {}
        scales = {}

        def transposes(job, x):
            tp = psum.tile([P, 2, 2 * P], F32, name="tp", tag="tp", bufs=3)
            for r in range(2):
                words = rows[job][2 * x + r].bitcast(F32)
                for u in range(2):
                    nc.tensor.transpose(tp[:, u, r * P : (r + 1) * P], words[:, u::2], ident[:])
            tps[(job, x)] = tp

        def copy_out(job, x, engine):
            if x == 0:
                grp = work.tile([P, 4 * P * 4], BF16, name="grp", tag="grp", bufs=3, align_bytes=256)
                grps[job] = grp
            grp_words = grps[job][:].bitcast(F32).rearrange("p (r u) -> p r u", u=2)
            dst = grp_words[:, x * 2 * P : (x + 1) * 2 * P, :]
            src = tps[(job, x)][:].rearrange("p u r -> p r u")
            if engine == "s":
                nc.scalar.copy(out=dst, in_=src)
            else:
                nc.vector.tensor_copy(out=dst, in_=src)

        def turn_bias():
            tb = psum.tile([P, 2, P], F32, name="tb", tag="tp", bufs=3)
            words = b1_rows[:].bitcast(F32)
            for u in range(2):
                nc.tensor.transpose(tb[:, u, :], words[:, u::2], ident[:])
            b1_words = b1_all[:].rearrange("p e t -> p (e t)").bitcast(F32).rearrange("p (e u) -> p e u", u=2)
            nc.vector.tensor_copy(out=b1_words, in_=tb[:, :, 0:EXPERTS].rearrange("p u e -> p e u"))

        def quantize_operand(job):
            c = keep.tile([P, 4 * P], U32, name="c_%s%d" % job, tag="c_%s%d" % job, align_bytes=256)
            s = keep.tile([P, 4 * P], U8, name="s_%s%d" % job, tag="s_%s%d" % job, align_bytes=256)
            nc.vector.quantize_mx(out=c[:].bitcast(FP8X4), scales=s[:], in_=grps[job][:])
            codes[job] = c
            scales[job] = s

        def quantize_half(job, x):
            if x == 0:
                c = keep.tile([P, 4 * P], U32, name="c_%s%d" % job, tag="c_%s%d" % job, align_bytes=256)
                s = keep.tile([P, 4 * P], U8, name="s_%s%d" % job, tag="s_%s%d" % job, align_bytes=256)
                codes[job] = c
                scales[job] = s
            cols = slice(x * 2 * P, (x + 1) * 2 * P)
            nc.vector.quantize_mx(out=codes[job][:, cols].bitcast(FP8X4), scales=scales[job][:, cols], in_=grps[job][:, x * 8 * P : (x + 1) * 8 * P])

        banks = {}
        zs = {}
        zis = {}
        h1c = {}
        h1s = {}
        ps2s = {}
        ys = {}
        acc = keep.tile([P, TILES, ACTIONS], F32, name="acc", tag="acc")
        o0_v = out_0.rearrange("(p i) a -> p i a", i=TILES)
        o1_v = out_1.rearrange("(p i) e a -> p i e a", i=TILES)

        def first_product(u):
            e, hf = u // 2, u % 2
            banks[u] = []
            for t in range(4):
                bank = psum.tile([P, HALF * P], BANK_DT, name="bank", tag="bank", bufs=3)
                nc.tensor.matmul_mx(
                    out=bank[:],
                    lhsT=codes[("w1", e)][:, t * P : (t + 1) * P].bitcast(FP8X4),
                    lhsT_scale=scales[("w1", e)][:, t * P : (t + 1) * P],
                    rhs=codes[("h", hf)][:].bitcast(FP8X4),
                    rhs_scale=scales[("h", hf)][:],
                    start=True,
                    stop=True,
                )
                banks[u].append(bank)

        def scalar_share(u):
            return LATE_S.get(u, S_SHARE) if u >= 2 else 0

        def bias_relu(u, engines):
            e = u // 2
            z = work.tile([P, 4, HALF * P], BF16, name="z", tag="z", bufs=3)
            for t in range(4):
                if engines[t] == "s":
                    nc.scalar.activation(out=z[:, t, :], in_=banks[u][t][:], func=ACT.Relu, bias=b1_col(e, t), scale=1.0)
                else:
                    nc.vector.tensor_scalar(out=z[:, t, :], in0=banks[u][t][:], scalar1=b1_col(e, t), scalar2=0.0, op0=ALU.add, op1=ALU.max)
            zs[u] = z
            zi = work.tile([P, HALF * P, 4], BF16, name="zi", tag="zi", bufs=3, align_bytes=256)
            zis[u] = zi
            lo = HALF * P - scalar_share(u)
            if lo < HALF * P:
                nc.scalar.copy(out=zi[:, lo:, :].rearrange("p (c i) t -> p c t i", i=RUN), in_=z[:, :, lo:].rearrange("p t (c i) -> p c t i", i=RUN))

        def interleave(u):
            lo = HALF * P - scalar_share(u)
            nc.vector.tensor_copy(out=zis[u][:, 0:lo, :].rearrange("p (c h i) t -> p h c t i", h=2, i=RUN), in_=zs[u][:, :, 0:lo].rearrange("p t (c h i) -> p h c t i", h=2, i=RUN))

        def quantize_h1(u):
            c = work.tile([P, HALF * P], U32, name="h1c", tag="h1c", bufs=UNITS, align_bytes=256)
            s = work.tile([P, HALF * P], U8, name="h1s", tag="h1s", bufs=UNITS, align_bytes=256)
            nc.vector.quantize_mx(out=c[:].bitcast(FP8X4), scales=s[:], in_=zis[u][:].rearrange("p n t -> p (n t)"))
            h1c[u] = c
            h1s[u] = s

        def second_product(u):
            e = u // 2
            w2 = ("w2", e // 4)
            cols = slice((e % 4) * P, (e % 4 + 1) * P)
            ps2 = psum.tile([P, HALF, ACTIONS], F32, name="ps2", tag="ps2", bufs=2)
            for j in range(HALF):
                nc.tensor.matmul_mx(
                    out=ps2[:, j, :],
                    lhsT=h1c[u][:, j * P : (j + 1) * P].bitcast(FP8X4),
                    lhsT_scale=h1s[u][:, j * P : (j + 1) * P],
                    rhs=codes[w2][:, cols].bitcast(FP8X4),
                    rhs_scale=scales[w2][:, cols],
                    start=True,
                    stop=True,
                )
            ps2s[u] = ps2

        def expert_out(u):
            e, hf = u // 2, u % 2
            y = work.tile([P, HALF, ACTIONS], F32, name="y", tag="y", bufs=UNITS)
            nc.vector.tensor_tensor(out=y[:], in0=ps2s[u][:], in1=b2bc[:, e : e + 1, :].to_broadcast([P, HALF, ACTIONS]), op=ALU.add)
            nc.sync.dma_start(out=o1_v[:, hf * HALF : (hf + 1) * HALF, e, :], in_=y[:])
            ys[u] = y

        def gate(u):
            e, hf = u // 2, u % 2
            for j in range(HALF):
                i = hf * HALF + j
                gcol = g8[:, i * EXPERTS + e : i * EXPERTS + e + 1]
                if e == 0:
                    nc.vector.tensor_scalar(out=acc[:, i, :], in0=ys[u][:, j, :], scalar1=gcol, scalar2=None, op0=ALU.mult)
                else:
                    nc.vector.scalar_tensor_tensor(out=acc[:, i, :], in0=ys[u][:, j, :], scalar=gcol, in1=acc[:, i, :], op0=ALU.mult, op1=ALU.add)

        def turn(job, engine):
            for x in range(2):
                transposes(job, x)
            if engine == "s":
                for x in range(2):
                    copy_out(job, x, "s")

        transposes(("h", 0), 0)
        copy_out(("h", 0), 0, "s")
        transposes(("h", 0), 1)
        copy_out(("h", 0), 1, "v")
        transposes(("w1", 0), 0)
        copy_out(("w1", 0), 0, "s")
        quantize_operand(("h", 0))
        quantize_half(("w1", 0), 0)
        transposes(("w1", 0), 1)
        copy_out(("w1", 0), 1, "v")
        turn(("h", 1), "s")
        quantize_half(("w1", 0), 1)
        first_product(0)
        quantize_operand(("h", 1))
        bias_relu(0, "ssvv")
        turn(("w1", 1), "s")
        first_product(1)
        bias_relu(1, "ssss")
        gates()

        early_at = {
            0: [(("w2", 0), 0, "v"), (("w2", 0), 1, "v")],
            1: [(("w1", 2), 0, "s"), (("w1", 2), 1, "s")],
            2: [(("w1", 3), 0, "s")],
            3: [(("w1", 3), 1, "s")],
            4: [(("w1", 4), 0, "s")],
            5: [(("w1", 4), 1, "s")],
            6: [(("w1", 5), 0, "s")],
            7: [(("w1", 5), 1, "s")],
            8: [(("w1", 6), 0, "s")],
            9: [(("w1", 6), 1, "s")],
            10: [(("w1", 7), 0, "s")],
            11: [(("w1", 7), 1, "s")],
        }
        late_at = {2: [(("w2", 1), 0, "s")], 4: [(("w2", 1), 1, "s")]}
        quant_at = {
            0: [("w1", 1)],
            1: [("w2", 0)],
            2: [("w1", 2)],
            4: [("w1", 3)],
            5: [("w2", 1)],
            6: [("w1", 4)],
            8: [("w1", 5)],
            10: [("w1", 6)],
            12: [("w1", 7)],
        }

        def half_jobs(jobs):
            for job, x, engine in jobs:
                transposes(job, x)
            for job, x, engine in jobs:
                if engine == "s":
                    copy_out(job, x, "s")

        for k in range(UNITS + 1):
            if 1 <= k < UNITS - 1:
                first_product(k + 1)
                bias_relu(k + 1, "ssss")
            half_jobs(early_at.get(k, []))
            if k == 0:
                turn_bias()
            if k < UNITS:
                interleave(k)
            for job in quant_at.get(k, []):
                quantize_operand(job)
            if k >= 2:
                expert_out(k - 2)
            if k < UNITS:
                quantize_h1(k)
            for job, x, engine in early_at.get(k, []):
                if engine == "v":
                    copy_out(job, x, "v")
            if k >= 2:
                gate(k - 2)
            if k >= 1:
                second_product(k - 1)
            half_jobs(late_at.get(k, []))
        nc.scalar.dma_start(out=o0_v[:, 0:HALF, :], in_=acc[:, 0:HALF, :])
        expert_out(UNITS - 1)
        gate(UNITS - 1)
        nc.scalar.dma_start(out=o0_v[:, HALF:TILES, :], in_=acc[:, HALF:TILES, :])
